import numpy as np
import ml_dtypes


def mxq(x, axis, fmt="e4m3"):
    dtype, down = {"e4m3": (ml_dtypes.float8_e4m3fn, 7), "e5m2": (ml_dtypes.float8_e5m2, 14)}[fmt]
    v = np.moveaxis(np.asarray(x, np.float32).astype(ml_dtypes.bfloat16).astype(np.float64), axis, -1)
    blocks = v.reshape(v.shape[:-1] + (-1, 32))
    amax = np.abs(blocks).max(-1, keepdims=True)
    byte = np.maximum(np.where(amax > 0, np.frexp(amax)[1] - 1 + 127, 0) - down, 1)
    scale = np.exp2(byte - 127.0)
    codes = (blocks / scale).astype(np.float32).astype(dtype).astype(np.float64)
    return np.moveaxis((codes * scale).reshape(v.shape), -1, axis)


WIDE = False


def mx_kscale(k):
    if not WIDE:
        return np.ones(k)
    levels = np.array([10, -10, 5, -5, 0])
    a = np.random.permutation(np.resize(levels, k // 512 * 4)).reshape(k // 512, 4)
    idx = np.arange(k)
    return np.exp2(a[idx // 512, idx % 128 // 32])


BF16 = ml_dtypes.bfloat16


def bf(x):
    return np.asarray(x, np.float32).astype(BF16)


def f64(x):
    return np.asarray(x).astype(np.float64)


B, S, DM, H, DH, QB = 1, 512, 512, 8, 128, 512
DI = H * DH
EPS_GN = 1e-5


def setup_inputs():
    s = mx_kscale(DI)
    h = np.random.standard_normal((B, S, H, DH)) * 0.15 + np.random.standard_normal((B, 1, H, 1)) * 0.15
    return {"h_attn": bf(h.reshape(B, S, DI)),
            "gn_w": bf((1.0 + 0.1 * np.random.standard_normal(DI)) * s),
            "gn_b": bf(0.1 * np.random.standard_normal(DI) * s),
            "W_out": bf(np.random.standard_normal((DM, DI)) / np.sqrt(DI) / s[None, :]),
            "x": bf(np.random.standard_normal((B, S, DM))),
            "skip_scale": bf(0.7 + 0.1 * np.random.standard_normal(1))}


def reference(h_attn, gn_w, gn_b, W_out, x, skip_scale):
    hg = f64(h_attn).reshape(B, S, H, DH)
    mu = hg.mean(axis=(1, 3), keepdims=True)
    var = hg.var(axis=(1, 3), keepdims=True)
    hg = (hg - mu) / np.sqrt(var + EPS_GN)
    h = hg.reshape(B, S, DI) * f64(gn_w) + f64(gn_b)
    return (mxq(h, 2, "e4m3") @ mxq(f64(W_out), 1, "e4m3").T) + f64(skip_scale) * f64(x)

@@ -1,0 +1,229 @@
+from contextlib import ExitStack
+
+import concourse.mybir as mybir
+from concourse.masks import make_identity
+
+FLOPS = 2 * 512 * 512 * 1024
+
+BF16 = mybir.dt.bfloat16
+F32 = mybir.dt.float32
+U32 = mybir.dt.uint32
+U8 = mybir.dt.uint8
+FP8X4 = mybir.dt.float8_e4m3fn_x4
+ALU = mybir.AluOpType
+ACT = mybir.ActivationFunctionType
+
+P = 128
+S = 512
+DM = 512
+ROWS = S // P
+PASSES = 2
+PAIRS = 4
+PAIR_CH = 256
+HEAD_CH = 128
+EPS_GN = 1e-5
+GROUP_SIZE = S * HEAD_CH
+W_BLOCKS = DM // P
+W_BANKS = 3
+HALF = S // 2
+
+
+def tile_mlstmblock_pb_s_kernel(tc, h_attn, gn_w, gn_b, W_out, x, skip_scale, out):
+    nc = tc.nc
+    h_rows = h_attn.flatten_outer_dims().rearrange("(p j) k -> p j k", j=ROWS)
+    x_rows = x.flatten_outer_dims().rearrange("(p j) m -> p j m", j=ROWS)
+    out_rows = out.flatten_outer_dims().rearrange("(p j) m -> p j m", j=ROWS)
+    w_rows = W_out.rearrange("(b p) k -> b p k", p=P)
+
+    with ExitStack() as ctx:
+        const = ctx.enter_context(tc.tile_pool(name="const", bufs=1))
+        data = ctx.enter_context(tc.tile_pool(name="data", bufs=1))
+        stat = ctx.enter_context(tc.tile_pool(name="stat", bufs=1))
+        psum = ctx.enter_context(tc.psum_pool(name="psum", bufs=1))
+        ctx.enter_context(tc.manual_schedule())
+
+        gn_src = const.tile([P, PAIR_CH], BF16)
+        nc.vector.memset(gn_src[:], 0.0)
+        nc.scalar.dma_start(out=gn_src[0:PAIRS, :], in_=gn_w.rearrange("(c w) -> c w", c=PAIRS))
+        nc.scalar.dma_start(out=gn_src[PAIRS : 2 * PAIRS, :], in_=gn_b.rearrange("(c w) -> c w", c=PAIRS))
+        skip_bf = const.tile([P, 1], BF16)
+        nc.scalar.dma_start(out=skip_bf[:], in_=skip_scale.partition_broadcast(P))
+
+        hx = []
+        for c in range(PAIRS):
+            hx_c = data.tile([P, ROWS, PAIR_CH], BF16, name="hx%d" % c)
+            nc.sync.dma_start(out=hx_c[:], in_=h_rows[:, :, PAIR_CH * c : PAIR_CH * (c + 1)])
+            hx.append(hx_c)
+        w_sb = []
+        for b in range(W_BLOCKS):
+            w_b = data.tile([P, PAIRS * PAIR_CH], BF16, name="w_sb%d" % b)
+            nc.sync.dma_start(out=w_b[:], in_=w_rows[b])
+            w_sb.append(w_b)
+        x_sb = data.tile([P, ROWS, DM], BF16)
+        nc.sync.dma_start(out=x_sb[:], in_=x_rows)
+
+        ident = const.tile([P, P], F32)
+        make_identity(nc, ident[:])
+        ones_col = const.tile([P, 2], BF16)
+        nc.vector.memset(ones_col[:], 1.0)
+        warm = const.tile([P, 1], F32)
+        nc.vector.memset(warm[:], 1.0)
+        warm_out = const.tile([P, 1], F32)
+        nc.scalar.activation(out=warm_out[:], in_=warm[:], func=ACT.Sqrt)
+        sel_even = const.tile([P, P], F32)
+        nc.vector.memset(sel_even[:, 0:64], 1.0 / GROUP_SIZE)
+        nc.vector.memset(sel_even[:, 64:P], 0.0)
+        sel_odd = const.tile([P, P], F32)
+        nc.vector.memset(sel_odd[:, 0:64], 0.0)
+        nc.vector.memset(sel_odd[:, 64:P], 1.0 / GROUP_SIZE)
+
+        small = psum.tile([P, 512], F32, tag="small")
+        gn_t = small[:, 0:P]
+        colsum = small[:, 128:144].rearrange("p (h n) -> p h n", n=2)
+        mean_sq = small[:, 384:388]
+        neg_mean = small[:, 388:392]
+
+        def transpose_pair(c):
+            h_t_c = psum.tile([P, S], F32, tag="h_t%d" % c, name="h_t%d" % c)
+            words = hx[c][:].bitcast(F32)
+            for j in range(ROWS):
+                nc.tensor.transpose(h_t_c[:, P * j : P * (j + 1)], words[:, j, :], ident[:])
+            return h_t_c
+
+        sq_even = stat.tile([P, PAIRS], F32)
+        sq_odd = stat.tile([P, PAIRS], F32)
+        junk_s = stat.tile([P, PAIRS, ROWS, HEAD_CH], BF16)
+        junk_v = stat.tile([P, PAIRS, ROWS, HEAD_CH], F32)
+        gn_wb = const.tile([P, 2 * PAIRS, 2], F32)
+        skip = const.tile([P, 1], F32)
+        h_t = [None] * PAIRS
+        for c in range(PAIRS):
+            for f in range(2):
+                for j in range(ROWS):
+                    nc.tensor.matmul(
+                        out=colsum[:, 2 * c + f, :],
+                        lhsT=hx[c][:, j, HEAD_CH * f : HEAD_CH * (f + 1)],
+                        rhs=ones_col[:],
+                        start=(j == 0),
+                        stop=(j == ROWS - 1),
+                    )
+            even = hx[c][:, :, 0:HEAD_CH]
+            odd = hx[c][:, :, HEAD_CH:PAIR_CH]
+            nc.scalar.activation(
+                out=junk_s[:, c], in_=even, func=ACT.Square, accum_out=sq_even[:, c : c + 1]
+            )
+            nc.vector.scalar_tensor_tensor(
+                out=junk_v[:, c], in0=odd, scalar=1.0, in1=odd, op0=ALU.mult, op1=ALU.mult,
+                accum_out=sq_odd[:, c : c + 1],
+            )
+            if c < PAIRS // PASSES:
+                h_t[c] = transpose_pair(c)
+            if c == 0:
+                nc.tensor.transpose(gn_t, gn_src[:].bitcast(F32), ident[:])
+            if c == 1:
+                nc.vector.tensor_copy(
+                    out=gn_wb[:],
+                    in_=small[:, 0 : 2 * PAIRS].bitcast(BF16).rearrange("q (r e) -> q r e", e=2),
+                )
+                nc.vector.tensor_copy(out=skip[:], in_=skip_bf[:])
+        gw = gn_wb[:, 0:PAIRS, :]
+        gb = gn_wb[:, PAIRS : 2 * PAIRS, :]
+
+        neg_colsum = stat.tile([P, 2, PAIRS], F32)
+        nc.vector.tensor_scalar(
+            out=neg_colsum[:], in0=colsum[:, :, 0].rearrange("p (c f) -> p f c", f=2),
+            scalar1=-1.0, scalar2=None, op0=ALU.mult,
+        )
+        h_t[2] = transpose_pair(2)
+        nc.tensor.matmul(out=mean_sq, lhsT=sel_even[:], rhs=sq_even[:], start=True, stop=False)
+        nc.tensor.matmul(out=mean_sq, lhsT=sel_odd[:], rhs=sq_odd[:], start=False, stop=True)
+        nc.tensor.matmul(out=neg_mean, lhsT=sel_even[:], rhs=neg_colsum[:, 0, :], start=True, stop=False)
+        nc.tensor.matmul(out=neg_mean, lhsT=sel_odd[:], rhs=neg_colsum[:, 1, :], start=False, stop=True)
+
+        sq_mean = stat.tile([P, PAIRS], F32)
+        nc.scalar.activation(out=sq_mean[:], in_=neg_mean, func=ACT.Square)
+        gw_neg_mean = stat.tile([P, PAIRS, 2], F32)
+        nc.vector.tensor_tensor(
+            out=gw_neg_mean[:], in0=gw, in1=neg_mean.unsqueeze(2).to_broadcast([P, PAIRS, 2]), op=ALU.mult
+        )
+        var_eps = stat.tile([P, PAIRS], F32)
+        nc.vector.scalar_tensor_tensor(
+            out=var_eps[:], in0=mean_sq, scalar=EPS_GN, in1=sq_mean[:], op0=ALU.add, op1=ALU.subtract
+        )
+        std = stat.tile([P, PAIRS], F32)
+        nc.scalar.activation(out=std[:], in_=var_eps[:], func=ACT.Sqrt)
+        rstd = stat.tile([P, PAIRS], F32)
+        nc.vector.reciprocal(out=rstd[:], in_=std[:])
+        rstd_b = rstd[:].unsqueeze(2).to_broadcast([P, PAIRS, 2])
+        shift_part = stat.tile([P, PAIRS, 2], F32)
+        nc.vector.tensor_tensor(out=shift_part[:], in0=gw_neg_mean[:], in1=rstd_b, op=ALU.mult)
+        scale = stat.tile([P, PAIRS, 2], F32)
+        nc.vector.tensor_tensor(out=scale[:], in0=gw, in1=rstd_b, op=ALU.mult)
+        shift = stat.tile([P, PAIRS, 2], F32)
+        nc.vector.tensor_tensor(out=shift[:], in0=shift_part[:], in1=gb, op=ALU.add)
+
+        w_grp = data.tile([P, PASSES, 4 * DM], BF16, align_bytes=64)
+        w_grp_words = w_grp[:].bitcast(F32).rearrange("q g (m u) -> q g m u", u=2)
+        w_codes = data.tile([P, PASSES, DM], U32, align_bytes=64)
+        w_scales = data.tile([P, PASSES, DM], U8, align_bytes=64)
+        for b in range(W_BLOCKS):
+            w_t = psum.tile([P, PAIRS, P], F32, tag="w_t%d" % (b % W_BANKS), name="w_t%d" % b)
+            words = w_sb[b][:].bitcast(F32)
+            for c in range(PAIRS):
+                nc.tensor.transpose(w_t[:, c, :], words[:, P * c : P * (c + 1)], ident[:])
+            copy_out = nc.scalar.copy if b < W_BLOCKS // 2 else nc.vector.tensor_copy
+            copy_out(
+                out=w_grp_words[:, :, P * b : P * (b + 1), :],
+                in_=w_t[:].rearrange("q (g u) m -> q g m u", u=2),
+            )
+        h_t[3] = transpose_pair(3)
+        for g in range(PASSES):
+            nc.vector.quantize_mx(
+                out=w_codes[:, g, :].bitcast(FP8X4), scales=w_scales[:, g, :], in_=w_grp[:, g, :]
+            )
+
+        h_codes = data.tile([P, PASSES, S], U32, align_bytes=64)
+        h_scales = data.tile([P, PASSES, S], U8, align_bytes=64)
+        acc_bank = ("w_t0", "w_t1", "w_t2", "h_t0")
+        acc = [None] * ROWS
+        for g in range(PASSES):
+            h_norm = data.tile([P, 4, S], BF16, name="h_norm%d" % g)
+            h_grp = data.tile([P, S, 4], BF16, name="h_grp%d" % g, align_bytes=64)
+            for half in range(2):
+                cols = slice(HALF * half, HALF * (half + 1))
+                for u in range(2):
+                    c = 2 * g + u
+                    halves = h_t[c][:].bitcast(BF16).rearrange("q (n e) -> q n e", e=2)
+                    for e in range(2):
+                        nc.scalar.activation(
+                            out=h_norm[:, 2 * u + e, cols], in_=halves[:, cols, e], func=ACT.Identity,
+                            scale=scale[:, c, e : e + 1], bias=shift[:, c, e : e + 1],
+                        )
+                nc.vector.tensor_copy(
+                    out=h_grp[:, cols, :].rearrange("q (c i) t -> q c t i", i=4),
+                    in_=h_norm[:, :, cols].rearrange("q t (c i) -> q c t i", i=4),
+                )
+                nc.vector.quantize_mx(
+                    out=h_codes[:, g, cols].bitcast(FP8X4), scales=h_scales[:, g, cols],
+                    in_=h_grp[:, cols, :].rearrange("q n t -> q (n t)"),
+                )
+                for j in range(2 * half, 2 * half + 2):
+                    if g == 0:
+                        acc[j] = psum.tile([P, DM], F32, tag=acc_bank[j], name="acc%d" % j)
+                    nc.tensor.matmul_mx(
+                        out=acc[j][:],
+                        lhsT=h_codes[:, g, P * j : P * (j + 1)].bitcast(FP8X4),
+                        lhsT_scale=h_scales[:, g, P * j : P * (j + 1)],
+                        rhs=w_codes[:, g, :].bitcast(FP8X4),
+                        rhs_scale=w_scales[:, g, :],
+                        start=(g == 0),
+                        stop=(g == PASSES - 1),
+                    )
+
+        out_sb = data.tile([P, ROWS, DM], F32)
+        for j in range(ROWS):
+            nc.vector.scalar_tensor_tensor(
+                out=out_sb[:, j, :], in0=x_sb[:, j, :], scalar=skip[:, 0:1], in1=acc[j][:],
+                op0=ALU.mult, op1=ALU.add,
+            )
+            nc.sync.dma_start(out=out_rows[:, j, :], in_=out_sb[:, j, :])

@@ -26,6 +26,7 @@ GROUP_SIZE = S * HEAD_CH
 W_BLOCKS = DM // P
 W_BANKS = 3
 HALF = S // 2
+SCALAR_PAIRS = 3
 
 
 def tile_mlstmblock_pb_s_kernel(tc, h_attn, gn_w, gn_b, W_out, x, skip_scale, out):
@@ -45,7 +46,7 @@ def tile_mlstmblock_pb_s_kernel(tc, h_attn, gn_w, gn_b, W_out, x, skip_scale, ou
         gn_src = const.tile([P, PAIR_CH], BF16)
         nc.vector.memset(gn_src[:], 0.0)
         nc.scalar.dma_start(out=gn_src[0:PAIRS, :], in_=gn_w.rearrange("(c w) -> c w", c=PAIRS))
-        nc.scalar.dma_start(out=gn_src[PAIRS : 2 * PAIRS, :], in_=gn_b.rearrange("(c w) -> c w", c=PAIRS))
+        nc.scalar.dma_start(out=gn_src[2 * PAIRS : 3 * PAIRS, :], in_=gn_b.rearrange("(c w) -> c w", c=PAIRS))
         skip_bf = const.tile([P, 1], BF16)
         nc.scalar.dma_start(out=skip_bf[:], in_=skip_scale.partition_broadcast(P))
 
@@ -64,24 +65,16 @@ def tile_mlstmblock_pb_s_kernel(tc, h_attn, gn_w, gn_b, W_out, x, skip_scale, ou
 
         ident = const.tile([P, P], F32)
         make_identity(nc, ident[:])
-        ones_col = const.tile([P, 2], BF16)
-        nc.vector.memset(ones_col[:], 1.0)
         warm = const.tile([P, 1], F32)
         nc.vector.memset(warm[:], 1.0)
         warm_out = const.tile([P, 1], F32)
-        nc.scalar.activation(out=warm_out[:], in_=warm[:], func=ACT.Sqrt)
-        sel_even = const.tile([P, P], F32)
-        nc.vector.memset(sel_even[:, 0:64], 1.0 / GROUP_SIZE)
-        nc.vector.memset(sel_even[:, 64:P], 0.0)
-        sel_odd = const.tile([P, P], F32)
-        nc.vector.memset(sel_odd[:, 0:64], 0.0)
-        nc.vector.memset(sel_odd[:, 64:P], 1.0 / GROUP_SIZE)
+        nc.scalar.activation(out=warm_out[:], in_=warm[:], func=ACT.Abs_reciprocal_sqrt)
+        averager = const.tile([P, P], F32)
+        nc.vector.memset(averager[:], 1.0 / GROUP_SIZE)
 
         small = psum.tile([P, 512], F32, tag="small")
         gn_t = small[:, 0:P]
-        colsum = small[:, 128:144].rearrange("p (h n) -> p h n", n=2)
-        mean_sq = small[:, 384:388]
-        neg_mean = small[:, 388:392]
+        means = small[:, 384:400].rearrange("p (k c f) -> p k c f", k=2, f=2)
 
         def transpose_pair(c):
             h_t_c = psum.tile([P, S], F32, tag="h_t%d" % c, name="h_t%d" % c)
@@ -90,93 +83,89 @@ def tile_mlstmblock_pb_s_kernel(tc, h_attn, gn_w, gn_b, W_out, x, skip_scale, ou
                 nc.tensor.transpose(h_t_c[:, P * j : P * (j + 1)], words[:, j, :], ident[:])
             return h_t_c
 
-        sq_even = stat.tile([P, PAIRS], F32)
-        sq_odd = stat.tile([P, PAIRS], F32)
-        junk_s = stat.tile([P, PAIRS, ROWS, HEAD_CH], BF16)
-        junk_v = stat.tile([P, PAIRS, ROWS, HEAD_CH], F32)
-        gn_wb = const.tile([P, 2 * PAIRS, 2], F32)
+        sums = stat.tile([P, 2, PAIRS, 8], F32)
+        junk_sq_s = stat.tile([P, 2 * SCALAR_PAIRS, ROWS, HEAD_CH], BF16)
+        junk_sq_v = stat.tile([P, 2 * (PAIRS - SCALAR_PAIRS), ROWS, HEAD_CH], F32)
+        junk_sum = stat.tile([P, 2 * PAIRS, ROWS, HEAD_CH], BF16)
+        gn_all = const.tile([P, 3, PAIRS, 2], F32)
         skip = const.tile([P, 1], F32)
-        h_t = [None] * PAIRS
+        h_t = []
         for c in range(PAIRS):
+            heads = [hx[c][:, :, HEAD_CH * f : HEAD_CH * (f + 1)] for f in range(2)]
             for f in range(2):
-                for j in range(ROWS):
-                    nc.tensor.matmul(
-                        out=colsum[:, 2 * c + f, :],
-                        lhsT=hx[c][:, j, HEAD_CH * f : HEAD_CH * (f + 1)],
-                        rhs=ones_col[:],
-                        start=(j == 0),
-                        stop=(j == ROWS - 1),
-                    )
-            even = hx[c][:, :, 0:HEAD_CH]
-            odd = hx[c][:, :, HEAD_CH:PAIR_CH]
-            nc.scalar.activation(
-                out=junk_s[:, c], in_=even, func=ACT.Square, accum_out=sq_even[:, c : c + 1]
-            )
-            nc.vector.scalar_tensor_tensor(
-                out=junk_v[:, c], in0=odd, scalar=1.0, in1=odd, op0=ALU.mult, op1=ALU.mult,
-                accum_out=sq_odd[:, c : c + 1],
-            )
-            if c < PAIRS // PASSES:
-                h_t[c] = transpose_pair(c)
-            if c == 0:
-                nc.tensor.transpose(gn_t, gn_src[:].bitcast(F32), ident[:])
-            if c == 1:
-                nc.vector.tensor_copy(
-                    out=gn_wb[:],
-                    in_=small[:, 0 : 2 * PAIRS].bitcast(BF16).rearrange("q (r e) -> q r e", e=2),
+                nc.vector.tensor_scalar(
+                    out=junk_sum[:, 2 * c + f], in0=heads[f], scalar1=-1.0, scalar2=None,
+                    op0=ALU.mult, op1=ALU.add, accum_out=sums[:, 0, c, f : f + 1],
                 )
-                nc.vector.tensor_copy(out=skip[:], in_=skip_bf[:])
-        gw = gn_wb[:, 0:PAIRS, :]
-        gb = gn_wb[:, PAIRS : 2 * PAIRS, :]
-
-        neg_colsum = stat.tile([P, 2, PAIRS], F32)
-        nc.vector.tensor_scalar(
-            out=neg_colsum[:], in0=colsum[:, :, 0].rearrange("p (c f) -> p f c", f=2),
-            scalar1=-1.0, scalar2=None, op0=ALU.mult,
+            for f in range(2):
+                if c < SCALAR_PAIRS:
+                    nc.scalar.activation(
+                        out=junk_sq_s[:, 2 * c + f], in_=heads[f], func=ACT.Square,
+                        accum_out=sums[:, 1, c, f : f + 1],
+                    )
+                else:
+                    nc.vector.scalar_tensor_tensor(
+                        out=junk_sq_v[:, 2 * (c - SCALAR_PAIRS) + f], in0=heads[f], scalar=1.0, in1=heads[f],
+                        op0=ALU.mult, op1=ALU.mult, accum_out=sums[:, 1, c, f : f + 1],
+                    )
+            h_t.append(transpose_pair(c))
+        nc.tensor.transpose(gn_t, gn_src[:].bitcast(F32), ident[:])
+        nc.vector.tensor_copy(
+            out=gn_all[:].rearrange("q a c e -> q (a c) e"),
+            in_=small[:, 0 : 3 * PAIRS].bitcast(BF16).rearrange("q (r e) -> q r e", e=2),
         )
-        h_t[2] = transpose_pair(2)
-        nc.tensor.matmul(out=mean_sq, lhsT=sel_even[:], rhs=sq_even[:], start=True, stop=False)
-        nc.tensor.matmul(out=mean_sq, lhsT=sel_odd[:], rhs=sq_odd[:], start=False, stop=True)
-        nc.tensor.matmul(out=neg_mean, lhsT=sel_even[:], rhs=neg_colsum[:, 0, :], start=True, stop=False)
-        nc.tensor.matmul(out=neg_mean, lhsT=sel_odd[:], rhs=neg_colsum[:, 1, :], start=False, stop=True)
-
-        sq_mean = stat.tile([P, PAIRS], F32)
-        nc.scalar.activation(out=sq_mean[:], in_=neg_mean, func=ACT.Square)
-        gw_neg_mean = stat.tile([P, PAIRS, 2], F32)
-        nc.vector.tensor_tensor(
-            out=gw_neg_mean[:], in0=gw, in1=neg_mean.unsqueeze(2).to_broadcast([P, PAIRS, 2]), op=ALU.mult
-        )
-        var_eps = stat.tile([P, PAIRS], F32)
-        nc.vector.scalar_tensor_tensor(
-            out=var_eps[:], in0=mean_sq, scalar=EPS_GN, in1=sq_mean[:], op0=ALU.add, op1=ALU.subtract
-        )
-        std = stat.tile([P, PAIRS], F32)
-        nc.scalar.activation(out=std[:], in_=var_eps[:], func=ACT.Sqrt)
-        rstd = stat.tile([P, PAIRS], F32)
-        nc.vector.reciprocal(out=rstd[:], in_=std[:])
-        rstd_b = rstd[:].unsqueeze(2).to_broadcast([P, PAIRS, 2])
-        shift_part = stat.tile([P, PAIRS, 2], F32)
-        nc.vector.tensor_tensor(out=shift_part[:], in0=gw_neg_mean[:], in1=rstd_b, op=ALU.mult)
-        scale = stat.tile([P, PAIRS, 2], F32)
-        nc.vector.tensor_tensor(out=scale[:], in0=gw, in1=rstd_b, op=ALU.mult)
-        shift = stat.tile([P, PAIRS, 2], F32)
-        nc.vector.tensor_tensor(out=shift[:], in0=shift_part[:], in1=gb, op=ALU.add)
+        nc.vector.tensor_copy(out=skip[:], in_=skip_bf[:])
+        gb = gn_all[:, 2]
 
         w_grp = data.tile([P, PASSES, 4 * DM], BF16, align_bytes=64)
         w_grp_words = w_grp[:].bitcast(F32).rearrange("q g (m u) -> q g m u", u=2)
-        w_codes = data.tile([P, PASSES, DM], U32, align_bytes=64)
-        w_scales = data.tile([P, PASSES, DM], U8, align_bytes=64)
-        for b in range(W_BLOCKS):
+
+        def transpose_w_block(b):
             w_t = psum.tile([P, PAIRS, P], F32, tag="w_t%d" % (b % W_BANKS), name="w_t%d" % b)
             words = w_sb[b][:].bitcast(F32)
             for c in range(PAIRS):
                 nc.tensor.transpose(w_t[:, c, :], words[:, P * c : P * (c + 1)], ident[:])
-            copy_out = nc.scalar.copy if b < W_BLOCKS // 2 else nc.vector.tensor_copy
-            copy_out(
+            nc.scalar.copy(
                 out=w_grp_words[:, :, P * b : P * (b + 1), :],
                 in_=w_t[:].rearrange("q (g u) m -> q g m u", u=2),
             )
-        h_t[3] = transpose_pair(3)
+
+        for b in range(W_BLOCKS // 2):
+            transpose_w_block(b)
+
+        nc.tensor.matmul(out=means, lhsT=averager[:], rhs=sums[:, :, :, 0:2], start=True, stop=True)
+        sq_mean = stat.tile([P, PAIRS], F32)
+        var_eps = stat.tile([P, PAIRS], F32)
+        for f in range(2):
+            rows = slice(64 * f, 64 * (f + 1))
+            nc.scalar.activation(out=sq_mean[rows, :], in_=means[rows, 0, :, f], func=ACT.Square)
+        for f in range(2):
+            rows = slice(64 * f, 64 * (f + 1))
+            nc.vector.tensor_tensor(
+                out=gn_all[rows, 1], in0=gn_all[rows, 0],
+                in1=means[rows, 0, :, f].unsqueeze(2).to_broadcast([64, PAIRS, 2]), op=ALU.mult,
+            )
+        for f in range(2):
+            rows = slice(64 * f, 64 * (f + 1))
+            nc.vector.scalar_tensor_tensor(
+                out=var_eps[rows, :], in0=means[rows, 1, :, f], scalar=EPS_GN, in1=sq_mean[rows, :],
+                op0=ALU.add, op1=ALU.subtract,
+            )
+        rstd = stat.tile([P, PAIRS], F32)
+        nc.scalar.activation(out=rstd[:], in_=var_eps[:], func=ACT.Abs_reciprocal_sqrt)
+        by_rstd = stat.tile([P, 2, PAIRS, 2], F32)
+        nc.vector.tensor_tensor(
+            out=by_rstd[:], in0=gn_all[:, 0:2],
+            in1=rstd[:].unsqueeze(1).unsqueeze(3).to_broadcast([P, 2, PAIRS, 2]), op=ALU.mult,
+        )
+        scale = by_rstd[:, 0]
+        shift = stat.tile([P, PAIRS, 2], F32)
+        nc.vector.tensor_tensor(out=shift[:], in0=by_rstd[:, 1], in1=gb, op=ALU.add)
+
+        for b in range(W_BLOCKS // 2, W_BLOCKS):
+            transpose_w_block(b)
+        w_codes = data.tile([P, PASSES, DM], U32, align_bytes=64)
+        w_scales = data.tile([P, PASSES, DM], U8, align_bytes=64)
         for g in range(PASSES):
             nc.vector.quantize_mx(
                 out=w_codes[:, g, :].bitcast(FP8X4), scales=w_scales[:, g, :], in_=w_grp[:, g, :]

@@ -26,6 +26,7 @@ GROUP_SIZE = S * HEAD_CH
 W_BLOCKS = DM // P
 W_BANKS = 3
 HALF = S // 2
+WARM_MATMULS = 3
 SCALAR_PAIRS = 3
 
 
@@ -69,6 +70,11 @@ def tile_mlstmblock_pb_s_kernel(tc, h_attn, gn_w, gn_b, W_out, x, skip_scale, ou
         nc.vector.memset(warm[:], 1.0)
         warm_out = const.tile([P, 1], F32)
         nc.scalar.activation(out=warm_out[:], in_=warm[:], func=ACT.Abs_reciprocal_sqrt)
+        warm_cols = const.tile([P, DM], BF16)
+        nc.vector.memset(warm_cols[:], 0.0)
+        warm_acc = psum.tile([P, DM], F32, tag="w_t0", name="warm_acc")
+        for i in range(WARM_MATMULS):
+            nc.tensor.matmul(out=warm_acc[:], lhsT=warm_cols[:, 0:P], rhs=warm_cols[:], start=True, stop=True)
         averager = const.tile([P, P], F32)
         nc.vector.memset(averager[:], 1.0 / GROUP_SIZE)
 

@@ -26,7 +26,6 @@ GROUP_SIZE = S * HEAD_CH
 W_BLOCKS = DM // P
 W_BANKS = 3
 HALF = S // 2
-WARM_MATMULS = 3
 SCALAR_PAIRS = 3
 
 
@@ -70,11 +69,6 @@ def tile_mlstmblock_pb_s_kernel(tc, h_attn, gn_w, gn_b, W_out, x, skip_scale, ou
         nc.vector.memset(warm[:], 1.0)
         warm_out = const.tile([P, 1], F32)
         nc.scalar.activation(out=warm_out[:], in_=warm[:], func=ACT.Abs_reciprocal_sqrt)
-        warm_cols = const.tile([P, DM], BF16)
-        nc.vector.memset(warm_cols[:], 0.0)
-        warm_acc = psum.tile([P, DM], F32, tag="w_t0", name="warm_acc")
-        for i in range(WARM_MATMULS):
-            nc.tensor.matmul(out=warm_acc[:], lhsT=warm_cols[:, 0:P], rhs=warm_cols[:], start=True, stop=True)
         averager = const.tile([P, P], F32)
         nc.vector.memset(averager[:], 1.0 / GROUP_SIZE)
 
@@ -95,7 +89,7 @@ def tile_mlstmblock_pb_s_kernel(tc, h_attn, gn_w, gn_b, W_out, x, skip_scale, ou
         junk_sum = stat.tile([P, 2 * PAIRS, ROWS, HEAD_CH], BF16)
         gn_all = const.tile([P, 3, PAIRS, 2], F32)
         skip = const.tile([P, 1], F32)
-        h_t = []
+        h_t = [None] * PAIRS
         for c in range(PAIRS):
             heads = [hx[c][:, :, HEAD_CH * f : HEAD_CH * (f + 1)] for f in range(2)]
             for f in range(2):
@@ -114,7 +108,8 @@ def tile_mlstmblock_pb_s_kernel(tc, h_attn, gn_w, gn_b, W_out, x, skip_scale, ou
                         out=junk_sq_v[:, 2 * (c - SCALAR_PAIRS) + f], in0=heads[f], scalar=1.0, in1=heads[f],
                         op0=ALU.mult, op1=ALU.mult, accum_out=sums[:, 1, c, f : f + 1],
                     )
-            h_t.append(transpose_pair(c))
+            if c < PAIRS // PASSES:
+                h_t[c] = transpose_pair(c)
         nc.tensor.transpose(gn_t, gn_src[:].bitcast(F32), ident[:])
         nc.vector.tensor_copy(
             out=gn_all[:].rearrange("q a c e -> q (a c) e"),
@@ -126,25 +121,39 @@ def tile_mlstmblock_pb_s_kernel(tc, h_attn, gn_w, gn_b, W_out, x, skip_scale, ou
         w_grp = data.tile([P, PASSES, 4 * DM], BF16, align_bytes=64)
         w_grp_words = w_grp[:].bitcast(F32).rearrange("q g (m u) -> q g m u", u=2)
 
+        w_t = [None] * W_BLOCKS
+
         def transpose_w_block(b):
-            w_t = psum.tile([P, PAIRS, P], F32, tag="w_t%d" % (b % W_BANKS), name="w_t%d" % b)
+            w_t[b] = psum.tile([P, PAIRS, P], F32, tag="w_t%d" % (b % W_BANKS), name="w_t%d" % b)
             words = w_sb[b][:].bitcast(F32)
             for c in range(PAIRS):
-                nc.tensor.transpose(w_t[:, c, :], words[:, P * c : P * (c + 1)], ident[:])
+                nc.tensor.transpose(w_t[b][:, c, :], words[:, P * c : P * (c + 1)], ident[:])
+
+        def copy_w_block(b):
             nc.scalar.copy(
                 out=w_grp_words[:, :, P * b : P * (b + 1), :],
-                in_=w_t[:].rearrange("q (g u) m -> q g m u", u=2),
+                in_=w_t[b][:].rearrange("q (g u) m -> q g m u", u=2),
             )
 
-        for b in range(W_BLOCKS // 2):
-            transpose_w_block(b)
+        transpose_w_block(0)
+        copy_w_block(0)
+        transpose_w_block(1)
+        copy_w_block(1)
+        transpose_w_block(2)
 
         nc.tensor.matmul(out=means, lhsT=averager[:], rhs=sums[:, :, :, 0:2], start=True, stop=True)
-        sq_mean = stat.tile([P, PAIRS], F32)
-        var_eps = stat.tile([P, PAIRS], F32)
-        for f in range(2):
-            rows = slice(64 * f, 64 * (f + 1))
-            nc.scalar.activation(out=sq_mean[rows, :], in_=means[rows, 0, :, f], func=ACT.Square)
+        sq_mean = stat.tile([P, PAIRS, 2], F32)
+        nc.scalar.activation(out=sq_mean[:], in_=means[:, 0], func=ACT.Square)
+        copy_w_block(2)
+        var_eps = stat.tile([P, PAIRS, 2], F32)
+        nc.vector.scalar_tensor_tensor(
+            out=var_eps[:], in0=means[:, 1], scalar=EPS_GN, in1=sq_mean[:], op0=ALU.add, op1=ALU.subtract
+        )
+        rstd = stat.tile([P, PAIRS, 2], F32)
+        nc.scalar.activation(out=rstd[:], in_=var_eps[:], func=ACT.Abs_reciprocal_sqrt)
+        transpose_w_block(3)
+        copy_w_block(3)
+        by_rstd = stat.tile([P, 2, PAIRS, 2], F32)
         for f in range(2):
             rows = slice(64 * f, 64 * (f + 1))
             nc.vector.tensor_tensor(
@@ -153,23 +162,16 @@ def tile_mlstmblock_pb_s_kernel(tc, h_attn, gn_w, gn_b, W_out, x, skip_scale, ou
             )
         for f in range(2):
             rows = slice(64 * f, 64 * (f + 1))
-            nc.vector.scalar_tensor_tensor(
-                out=var_eps[rows, :], in0=means[rows, 1, :, f], scalar=EPS_GN, in1=sq_mean[rows, :],
-                op0=ALU.add, op1=ALU.subtract,
+            nc.vector.tensor_tensor(
+                out=by_rstd[rows], in0=gn_all[rows, 0:2],
+                in1=rstd[rows, :, f].unsqueeze(1).unsqueeze(3).to_broadcast([64, 2, PAIRS, 2]), op=ALU.mult,
             )
-        rstd = stat.tile([P, PAIRS], F32)
-        nc.scalar.activation(out=rstd[:], in_=var_eps[:], func=ACT.Abs_reciprocal_sqrt)
-        by_rstd = stat.tile([P, 2, PAIRS, 2], F32)
-        nc.vector.tensor_tensor(
-            out=by_rstd[:], in0=gn_all[:, 0:2],
-            in1=rstd[:].unsqueeze(1).unsqueeze(3).to_broadcast([P, 2, PAIRS, 2]), op=ALU.mult,
-        )
         scale = by_rstd[:, 0]
         shift = stat.tile([P, PAIRS, 2], F32)
         nc.vector.tensor_tensor(out=shift[:], in0=by_rstd[:, 1], in1=gb, op=ALU.add)
 
-        for b in range(W_BLOCKS // 2, W_BLOCKS):
-            transpose_w_block(b)
+        for c in range(PAIRS // PASSES, PAIRS):
+            h_t[c] = transpose_pair(c)
         w_codes = data.tile([P, PASSES, DM], U32, align_bytes=64)
         w_scales = data.tile([P, PASSES, DM], U8, align_bytes=64)
         for g in range(PASSES):

@@ -43,18 +43,15 @@ def tile_mlstmblock_pb_s_kernel(tc, h_attn, gn_w, gn_b, W_out, x, skip_scale, ou
         psum = ctx.enter_context(tc.psum_pool(name="psum", bufs=1))
         ctx.enter_context(tc.manual_schedule())
 
-        gn_src = const.tile([P, PAIR_CH], BF16)
-        nc.vector.memset(gn_src[:], 0.0)
-        nc.scalar.dma_start(out=gn_src[0:PAIRS, :], in_=gn_w.rearrange("(c w) -> c w", c=PAIRS))
-        nc.scalar.dma_start(out=gn_src[2 * PAIRS : 3 * PAIRS, :], in_=gn_b.rearrange("(c w) -> c w", c=PAIRS))
-        skip_bf = const.tile([P, 1], BF16)
-        nc.scalar.dma_start(out=skip_bf[:], in_=skip_scale.partition_broadcast(P))
-
         hx = []
         for c in range(PAIRS):
             hx_c = data.tile([P, ROWS, PAIR_CH], BF16, name="hx%d" % c)
             nc.sync.dma_start(out=hx_c[:], in_=h_rows[:, :, PAIR_CH * c : PAIR_CH * (c + 1)])
             hx.append(hx_c)
+        gn_src = const.tile([P, PAIR_CH], BF16)
+        nc.vector.memset(gn_src[:], 0.0)
+        nc.sync.dma_start(out=gn_src[0:PAIRS, :], in_=gn_w.rearrange("(c w) -> c w", c=PAIRS))
+        nc.sync.dma_start(out=gn_src[PAIRS : 2 * PAIRS, :], in_=gn_b.rearrange("(c w) -> c w", c=PAIRS))
         w_sb = []
         for b in range(W_BLOCKS):
             w_b = data.tile([P, PAIRS * PAIR_CH], BF16, name="w_sb%d" % b)
@@ -62,6 +59,8 @@ def tile_mlstmblock_pb_s_kernel(tc, h_attn, gn_w, gn_b, W_out, x, skip_scale, ou
             w_sb.append(w_b)
         x_sb = data.tile([P, ROWS, DM], BF16)
         nc.sync.dma_start(out=x_sb[:], in_=x_rows)
+        skip_bf = const.tile([P, 1], BF16)
+        nc.sync.dma_start(out=skip_bf[:], in_=skip_scale.partition_broadcast(P))
 
         ident = const.tile([P, P], F32)
         make_identity(nc, ident[:])
@@ -87,8 +86,9 @@ def tile_mlstmblock_pb_s_kernel(tc, h_attn, gn_w, gn_b, W_out, x, skip_scale, ou
         junk_sq_s = stat.tile([P, 2 * SCALAR_PAIRS, ROWS, HEAD_CH], BF16)
         junk_sq_v = stat.tile([P, 2 * (PAIRS - SCALAR_PAIRS), ROWS, HEAD_CH], F32)
         junk_sum = stat.tile([P, 2 * PAIRS, ROWS, HEAD_CH], BF16)
-        gn_all = const.tile([P, 3, PAIRS, 2], F32)
-        skip = const.tile([P, 1], F32)
+        factors = const.tile([P, PAIRS, 2, 2], F32)
+        offsets = const.tile([P, PAIRS, 2, 2], F32)
+        nc.vector.memset(offsets[:], 0.0)
         h_t = [None] * PAIRS
         for c in range(PAIRS):
             heads = [hx[c][:, :, HEAD_CH * f : HEAD_CH * (f + 1)] for f in range(2)]
@@ -110,13 +110,6 @@ def tile_mlstmblock_pb_s_kernel(tc, h_attn, gn_w, gn_b, W_out, x, skip_scale, ou
                     )
             if c < PAIRS // PASSES:
                 h_t[c] = transpose_pair(c)
-        nc.tensor.transpose(gn_t, gn_src[:].bitcast(F32), ident[:])
-        nc.vector.tensor_copy(
-            out=gn_all[:].rearrange("q a c e -> q (a c) e"),
-            in_=small[:, 0 : 3 * PAIRS].bitcast(BF16).rearrange("q (r e) -> q r e", e=2),
-        )
-        nc.vector.tensor_copy(out=skip[:], in_=skip_bf[:])
-        gb = gn_all[:, 2]
 
         w_grp = data.tile([P, PASSES, 4 * DM], BF16, align_bytes=64)
         w_grp_words = w_grp[:].bitcast(F32).rearrange("q g (m u) -> q g m u", u=2)
@@ -139,36 +132,39 @@ def tile_mlstmblock_pb_s_kernel(tc, h_attn, gn_w, gn_b, W_out, x, skip_scale, ou
         copy_w_block(0)
         transpose_w_block(1)
         copy_w_block(1)
+        nc.tensor.transpose(gn_t, gn_src[:].bitcast(F32), ident[:])
+        gn_cols = small[:, 0 : 2 * PAIRS].bitcast(BF16).rearrange("q (r e) -> q r e", e=2)
+        nc.vector.tensor_copy(out=factors[:, :, 0, :], in_=gn_cols[:, 0:PAIRS, :])
+        nc.vector.tensor_copy(out=offsets[:, :, 1, :], in_=gn_cols[:, PAIRS : 2 * PAIRS, :])
         transpose_w_block(2)
 
         nc.tensor.matmul(out=means, lhsT=averager[:], rhs=sums[:, :, :, 0:2], start=True, stop=True)
         sq_mean = stat.tile([P, PAIRS, 2], F32)
         nc.scalar.activation(out=sq_mean[:], in_=means[:, 0], func=ACT.Square)
         copy_w_block(2)
-        var_eps = stat.tile([P, PAIRS, 2], F32)
-        nc.vector.scalar_tensor_tensor(
-            out=var_eps[:], in0=means[:, 1], scalar=EPS_GN, in1=sq_mean[:], op0=ALU.add, op1=ALU.subtract
-        )
-        rstd = stat.tile([P, PAIRS, 2], F32)
-        nc.scalar.activation(out=rstd[:], in_=var_eps[:], func=ACT.Abs_reciprocal_sqrt)
-        transpose_w_block(3)
-        copy_w_block(3)
-        by_rstd = stat.tile([P, 2, PAIRS, 2], F32)
+        var_eps = stat.tile([P, PAIRS], F32)
         for f in range(2):
             rows = slice(64 * f, 64 * (f + 1))
             nc.vector.tensor_tensor(
-                out=gn_all[rows, 1], in0=gn_all[rows, 0],
+                out=factors[rows, :, 1, :], in0=factors[rows, :, 0, :],
                 in1=means[rows, 0, :, f].unsqueeze(2).to_broadcast([64, PAIRS, 2]), op=ALU.mult,
             )
         for f in range(2):
             rows = slice(64 * f, 64 * (f + 1))
-            nc.vector.tensor_tensor(
-                out=by_rstd[rows], in0=gn_all[rows, 0:2],
-                in1=rstd[rows, :, f].unsqueeze(1).unsqueeze(3).to_broadcast([64, 2, PAIRS, 2]), op=ALU.mult,
+            nc.vector.scalar_tensor_tensor(
+                out=var_eps[rows, :], in0=means[rows, 1, :, f], scalar=EPS_GN, in1=sq_mean[rows, :, f],
+                op0=ALU.add, op1=ALU.subtract,
             )
-        scale = by_rstd[:, 0]
-        shift = stat.tile([P, PAIRS, 2], F32)
-        nc.vector.tensor_tensor(out=shift[:], in0=by_rstd[:, 1], in1=gb, op=ALU.add)
+        rstd = stat.tile([P, PAIRS], F32)
+        nc.scalar.activation(out=rstd[:], in_=var_eps[:], func=ACT.Abs_reciprocal_sqrt)
+        transpose_w_block(3)
+        copy_w_block(3)
+        affine = stat.tile([P, PAIRS, 2, 2], F32)
+        for c in range(PAIRS):
+            nc.vector.scalar_tensor_tensor(
+                out=affine[:, c], in0=factors[:, c], scalar=rstd[:, c : c + 1], in1=offsets[:, c],
+                op0=ALU.mult, op1=ALU.add,
+            )
 
         for c in range(PAIRS // PASSES, PAIRS):
             h_t[c] = transpose_pair(c)
@@ -194,7 +190,7 @@ def tile_mlstmblock_pb_s_kernel(tc, h_attn, gn_w, gn_b, W_out, x, skip_scale, ou
                     for e in range(2):
                         nc.scalar.activation(
                             out=h_norm[:, 2 * u + e, cols], in_=halves[:, cols, e], func=ACT.Identity,
-                            scale=scale[:, c, e : e + 1], bias=shift[:, c, e : e + 1],
+                            scale=affine[:, c, 0, e : e + 1], bias=affine[:, c, 1, e : e + 1],
                         )
                 nc.vector.tensor_copy(
                     out=h_grp[:, cols, :].rearrange("q (c i) t -> q c t i", i=4),
@@ -220,7 +216,7 @@ def tile_mlstmblock_pb_s_kernel(tc, h_attn, gn_w, gn_b, W_out, x, skip_scale, ou
         out_sb = data.tile([P, ROWS, DM], F32)
         for j in range(ROWS):
             nc.vector.scalar_tensor_tensor(
-                out=out_sb[:, j, :], in0=x_sb[:, j, :], scalar=skip[:, 0:1], in1=acc[j][:],
+                out=out_sb[:, j, :], in0=x_sb[:, j, :], scalar=skip_bf[:, 0:1], in1=acc[j][:],
                 op0=ALU.mult, op1=ALU.add,
             )
             nc.sync.dma_start(out=out_rows[:, j, :], in_=out_sb[:, j, :])

@@ -43,15 +43,16 @@ def tile_mlstmblock_pb_s_kernel(tc, h_attn, gn_w, gn_b, W_out, x, skip_scale, ou
         psum = ctx.enter_context(tc.psum_pool(name="psum", bufs=1))
         ctx.enter_context(tc.manual_schedule())
 
+        gn_src = const.tile([P, PAIR_CH], BF16)
+        nc.vector.memset(gn_src[:], 0.0)
+        nc.scalar.dma_start(out=gn_src[0:PAIRS, :], in_=gn_w.rearrange("(c w) -> c w", c=PAIRS))
+        nc.scalar.dma_start(out=gn_src[PAIRS : 2 * PAIRS, :], in_=gn_b.rearrange("(c w) -> c w", c=PAIRS))
+
         hx = []
         for c in range(PAIRS):
             hx_c = data.tile([P, ROWS, PAIR_CH], BF16, name="hx%d" % c)
             nc.sync.dma_start(out=hx_c[:], in_=h_rows[:, :, PAIR_CH * c : PAIR_CH * (c + 1)])
             hx.append(hx_c)
-        gn_src = const.tile([P, PAIR_CH], BF16)
-        nc.vector.memset(gn_src[:], 0.0)
-        nc.sync.dma_start(out=gn_src[0:PAIRS, :], in_=gn_w.rearrange("(c w) -> c w", c=PAIRS))
-        nc.sync.dma_start(out=gn_src[PAIRS : 2 * PAIRS, :], in_=gn_b.rearrange("(c w) -> c w", c=PAIRS))
         w_sb = []
         for b in range(W_BLOCKS):
             w_b = data.tile([P, PAIRS * PAIR_CH], BF16, name="w_sb%d" % b)
@@ -110,6 +111,10 @@ def tile_mlstmblock_pb_s_kernel(tc, h_attn, gn_w, gn_b, W_out, x, skip_scale, ou
                     )
             if c < PAIRS // PASSES:
                 h_t[c] = transpose_pair(c)
+        nc.tensor.transpose(gn_t, gn_src[:].bitcast(F32), ident[:])
+        gn_cols = small[:, 0 : 2 * PAIRS].bitcast(BF16).rearrange("q (r e) -> q r e", e=2)
+        nc.vector.tensor_copy(out=factors[:, :, 0, :], in_=gn_cols[:, 0:PAIRS, :])
+        nc.vector.tensor_copy(out=offsets[:, :, 1, :], in_=gn_cols[:, PAIRS : 2 * PAIRS, :])
 
         w_grp = data.tile([P, PASSES, 4 * DM], BF16, align_bytes=64)
         w_grp_words = w_grp[:].bitcast(F32).rearrange("q g (m u) -> q g m u", u=2)
@@ -132,10 +137,6 @@ def tile_mlstmblock_pb_s_kernel(tc, h_attn, gn_w, gn_b, W_out, x, skip_scale, ou
         copy_w_block(0)
         transpose_w_block(1)
         copy_w_block(1)
-        nc.tensor.transpose(gn_t, gn_src[:].bitcast(F32), ident[:])
-        gn_cols = small[:, 0 : 2 * PAIRS].bitcast(BF16).rearrange("q (r e) -> q r e", e=2)
-        nc.vector.tensor_copy(out=factors[:, :, 0, :], in_=gn_cols[:, 0:PAIRS, :])
-        nc.vector.tensor_copy(out=offsets[:, :, 1, :], in_=gn_cols[:, PAIRS : 2 * PAIRS, :])
         transpose_w_block(2)
 
         nc.tensor.matmul(out=means, lhsT=averager[:], rhs=sums[:, :, :, 0:2], start=True, stop=True)
@@ -213,10 +214,12 @@ def tile_mlstmblock_pb_s_kernel(tc, h_attn, gn_w, gn_b, W_out, x, skip_scale, ou
                         stop=(g == PASSES - 1),
                     )
 
+        skip = const.tile([P, 1], F32)
+        nc.gpsimd.tensor_copy(out=skip[:], in_=skip_bf[:])
         out_sb = data.tile([P, ROWS, DM], F32)
         for j in range(ROWS):
             nc.vector.scalar_tensor_tensor(
-                out=out_sb[:, j, :], in0=x_sb[:, j, :], scalar=skip_bf[:, 0:1], in1=acc[j][:],
+                out=out_sb[:, j, :], in0=x_sb[:, j, :], scalar=skip[:, 0:1], in1=acc[j][:],
                 op0=ALU.mult, op1=ALU.add,
             )
             nc.sync.dma_start(out=out_rows[:, j, :], in_=out_sb[:, j, :])

from contextlib import ExitStack

import concourse.mybir as mybir
from concourse.masks import make_identity

FLOPS = 2 * 512 * 512 * 1024

BF16 = mybir.dt.bfloat16
F32 = mybir.dt.float32
U32 = mybir.dt.uint32
U8 = mybir.dt.uint8
FP8X4 = mybir.dt.float8_e4m3fn_x4
ALU = mybir.AluOpType
ACT = mybir.ActivationFunctionType

P = 128
S = 512
DM = 512
ROWS = S // P
PASSES = 2
PAIRS = 4
PAIR_CH = 256
HEAD_CH = 128
EPS_GN = 1e-5
GROUP_SIZE = S * HEAD_CH
W_BLOCKS = DM // P
W_BANKS = 3
HALF = S // 2
SCALAR_PAIRS = 3


def tile_mlstmblock_pb_s_kernel(tc, h_attn, gn_w, gn_b, W_out, x, skip_scale, out):
    nc = tc.nc
    h_rows = h_attn.flatten_outer_dims().rearrange("(p j) k -> p j k", j=ROWS)
    x_rows = x.flatten_outer_dims().rearrange("(p j) m -> p j m", j=ROWS)
    out_rows = out.flatten_outer_dims().rearrange("(p j) m -> p j m", j=ROWS)
    w_rows = W_out.rearrange("(b p) k -> b p k", p=P)

    with ExitStack() as ctx:
        const = ctx.enter_context(tc.tile_pool(name="const", bufs=1))
        data = ctx.enter_context(tc.tile_pool(name="data", bufs=1))
        stat = ctx.enter_context(tc.tile_pool(name="stat", bufs=1))
        psum = ctx.enter_context(tc.psum_pool(name="psum", bufs=1))
        ctx.enter_context(tc.manual_schedule())

        gn_src = const.tile([P, PAIR_CH], BF16)
        nc.vector.memset(gn_src[:], 0.0)
        nc.scalar.dma_start(out=gn_src[0:PAIRS, :], in_=gn_w.rearrange("(c w) -> c w", c=PAIRS))
        nc.scalar.dma_start(out=gn_src[PAIRS : 2 * PAIRS, :], in_=gn_b.rearrange("(c w) -> c w", c=PAIRS))

        hx = []
        for c in range(PAIRS):
            hx_c = data.tile([P, ROWS, PAIR_CH], BF16, name="hx%d" % c)
            nc.sync.dma_start(out=hx_c[:], in_=h_rows[:, :, PAIR_CH * c : PAIR_CH * (c + 1)])
            hx.append(hx_c)
        w_sb = []
        for b in range(W_BLOCKS):
            w_b = data.tile([P, PAIRS * PAIR_CH], BF16, name="w_sb%d" % b)
            nc.sync.dma_start(out=w_b[:], in_=w_rows[b])
            w_sb.append(w_b)
        x_sb = data.tile([P, ROWS, DM], BF16)
        nc.sync.dma_start(out=x_sb[:], in_=x_rows)
        skip_bf = const.tile([P, 1], BF16)
        nc.sync.dma_start(out=skip_bf[:], in_=skip_scale.partition_broadcast(P))

        ident = const.tile([P, P], F32)
        make_identity(nc, ident[:])
        warm = const.tile([P, 1], F32)
        nc.vector.memset(warm[:], 1.0)
        warm_out = const.tile([P, 1], F32)
        nc.scalar.activation(out=warm_out[:], in_=warm[:], func=ACT.Abs_reciprocal_sqrt)
        averager = const.tile([P, P], F32)
        nc.vector.memset(averager[:], 1.0 / GROUP_SIZE)

        small = psum.tile([P, 512], F32, tag="small")
        gn_t = small[:, 0:P]
        means = small[:, 384:400].rearrange("p (k c f) -> p k c f", k=2, f=2)

        def transpose_pair(c):
            h_t_c = psum.tile([P, S], F32, tag="h_t%d" % c, name="h_t%d" % c)
            words = hx[c][:].bitcast(F32)
            for j in range(ROWS):
                nc.tensor.transpose(h_t_c[:, P * j : P * (j + 1)], words[:, j, :], ident[:])
            return h_t_c

        sums = stat.tile([P, 2, PAIRS, 8], F32)
        junk_sq_s = stat.tile([P, 2 * SCALAR_PAIRS, ROWS, HEAD_CH], BF16)
        junk_sq_v = stat.tile([P, 2 * (PAIRS - SCALAR_PAIRS), ROWS, HEAD_CH], F32)
        junk_sum = stat.tile([P, 2 * PAIRS, ROWS, HEAD_CH], BF16)
        factors = const.tile([P, PAIRS, 2, 2], F32)
        offsets = const.tile([P, PAIRS, 2, 2], F32)
        nc.vector.memset(offsets[:], 0.0)
        h_t = [None] * PAIRS
        for c in range(PAIRS):
            heads = [hx[c][:, :, HEAD_CH * f : HEAD_CH * (f + 1)] for f in range(2)]
            for f in range(2):
                nc.vector.tensor_scalar(
                    out=junk_sum[:, 2 * c + f], in0=heads[f], scalar1=-1.0, scalar2=None,
                    op0=ALU.mult, op1=ALU.add, accum_out=sums[:, 0, c, f : f + 1],
                )
            for f in range(2):
                if c < SCALAR_PAIRS:
                    nc.scalar.activation(
                        out=junk_sq_s[:, 2 * c + f], in_=heads[f], func=ACT.Square,
                        accum_out=sums[:, 1, c, f : f + 1],
                    )
                else:
                    nc.vector.scalar_tensor_tensor(
                        out=junk_sq_v[:, 2 * (c - SCALAR_PAIRS) + f], in0=heads[f], scalar=1.0, in1=heads[f],
                        op0=ALU.mult, op1=ALU.mult, accum_out=sums[:, 1, c, f : f + 1],
                    )
            if c < PAIRS // PASSES:
                h_t[c] = transpose_pair(c)
        nc.tensor.transpose(gn_t, gn_src[:].bitcast(F32), ident[:])
        gn_cols = small[:, 0 : 2 * PAIRS].bitcast(BF16).rearrange("q (r e) -> q r e", e=2)
        nc.vector.tensor_copy(out=factors[:, :, 0, :], in_=gn_cols[:, 0:PAIRS, :])
        nc.vector.tensor_copy(out=offsets[:, :, 1, :], in_=gn_cols[:, PAIRS : 2 * PAIRS, :])

        w_grp = data.tile([P, PASSES, 4 * DM], BF16, align_bytes=64)
        w_grp_words = w_grp[:].bitcast(F32).rearrange("q g (m u) -> q g m u", u=2)

        w_t = [None] * W_BLOCKS

        def transpose_w_block(b):
            w_t[b] = psum.tile([P, PAIRS, P], F32, tag="w_t%d" % (b % W_BANKS), name="w_t%d" % b)
            words = w_sb[b][:].bitcast(F32)
            for c in range(PAIRS):
                nc.tensor.transpose(w_t[b][:, c, :], words[:, P * c : P * (c + 1)], ident[:])

        def copy_w_block(b):
            nc.scalar.copy(
                out=w_grp_words[:, :, P * b : P * (b + 1), :],
                in_=w_t[b][:].rearrange("q (g u) m -> q g m u", u=2),
            )

        transpose_w_block(0)
        copy_w_block(0)
        transpose_w_block(1)
        copy_w_block(1)
        transpose_w_block(2)

        nc.tensor.matmul(out=means, lhsT=averager[:], rhs=sums[:, :, :, 0:2], start=True, stop=True)
        sq_mean = stat.tile([P, PAIRS, 2], F32)
        nc.scalar.activation(out=sq_mean[:], in_=means[:, 0], func=ACT.Square)
        copy_w_block(2)
        var_eps = stat.tile([P, PAIRS], F32)
        for f in range(2):
            rows = slice(64 * f, 64 * (f + 1))
            nc.vector.tensor_tensor(
                out=factors[rows, :, 1, :], in0=factors[rows, :, 0, :],
                in1=means[rows, 0, :, f].unsqueeze(2).to_broadcast([64, PAIRS, 2]), op=ALU.mult,
            )
        for f in range(2):
            rows = slice(64 * f, 64 * (f + 1))
            nc.vector.scalar_tensor_tensor(
                out=var_eps[rows, :], in0=means[rows, 1, :, f], scalar=EPS_GN, in1=sq_mean[rows, :, f],
                op0=ALU.add, op1=ALU.subtract,
            )
        rstd = stat.tile([P, PAIRS], F32)
        nc.scalar.activation(out=rstd[:], in_=var_eps[:], func=ACT.Abs_reciprocal_sqrt)
        transpose_w_block(3)
        copy_w_block(3)
        affine = stat.tile([P, PAIRS, 2, 2], F32)
        for c in range(PAIRS):
            nc.vector.scalar_tensor_tensor(
                out=affine[:, c], in0=factors[:, c], scalar=rstd[:, c : c + 1], in1=offsets[:, c],
                op0=ALU.mult, op1=ALU.add,
            )

        for c in range(PAIRS // PASSES, PAIRS):
            h_t[c] = transpose_pair(c)
        w_codes = data.tile([P, PASSES, DM], U32, align_bytes=64)
        w_scales = data.tile([P, PASSES, DM], U8, align_bytes=64)
        for g in range(PASSES):
            nc.vector.quantize_mx(
                out=w_codes[:, g, :].bitcast(FP8X4), scales=w_scales[:, g, :], in_=w_grp[:, g, :]
            )

        h_codes = data.tile([P, PASSES, S], U32, align_bytes=64)
        h_scales = data.tile([P, PASSES, S], U8, align_bytes=64)
        acc_bank = ("w_t0", "w_t1", "w_t2", "h_t0")
        acc = [None] * ROWS
        for g in range(PASSES):
            h_norm = data.tile([P, 4, S], BF16, name="h_norm%d" % g)
            h_grp = data.tile([P, S, 4], BF16, name="h_grp%d" % g, align_bytes=64)
            for half in range(2):
                cols = slice(HALF * half, HALF * (half + 1))
                for u in range(2):
                    c = 2 * g + u
                    halves = h_t[c][:].bitcast(BF16).rearrange("q (n e) -> q n e", e=2)
                    for e in range(2):
                        nc.scalar.activation(
                            out=h_norm[:, 2 * u + e, cols], in_=halves[:, cols, e], func=ACT.Identity,
                            scale=affine[:, c, 0, e : e + 1], bias=affine[:, c, 1, e : e + 1],
                        )
                nc.vector.tensor_copy(
                    out=h_grp[:, cols, :].rearrange("q (c i) t -> q c t i", i=4),
                    in_=h_norm[:, :, cols].rearrange("q t (c i) -> q c t i", i=4),
                )
                nc.vector.quantize_mx(
                    out=h_codes[:, g, cols].bitcast(FP8X4), scales=h_scales[:, g, cols],
                    in_=h_grp[:, cols, :].rearrange("q n t -> q (n t)"),
                )
                for j in range(2 * half, 2 * half + 2):
                    if g == 0:
                        acc[j] = psum.tile([P, DM], F32, tag=acc_bank[j], name="acc%d" % j)
                    nc.tensor.matmul_mx(
                        out=acc[j][:],
                        lhsT=h_codes[:, g, P * j : P * (j + 1)].bitcast(FP8X4),
                        lhsT_scale=h_scales[:, g, P * j : P * (j + 1)],
                        rhs=w_codes[:, g, :].bitcast(FP8X4),
                        rhs_scale=w_scales[:, g, :],
                        start=(g == 0),
                        stop=(g == PASSES - 1),
                    )

        skip = const.tile([P, 1], F32)
        nc.gpsimd.tensor_copy(out=skip[:], in_=skip_bf[:])
        out_sb = data.tile([P, ROWS, DM], F32)
        for j in range(ROWS):
            nc.vector.scalar_tensor_tensor(
                out=out_sb[:, j, :], in0=x_sb[:, j, :], scalar=skip[:, 0:1], in1=acc[j][:],
                op0=ALU.mult, op1=ALU.add,
            )
            nc.sync.dma_start(out=out_rows[:, j, :], in_=out_sb[:, j, :])
